import numpy as np
import ml_dtypes

BF16 = ml_dtypes.bfloat16


def bf(x):
    return np.asarray(x, np.float32).astype(BF16)


def f32(x):
    return np.asarray(x, np.float32)


def f64(x):
    return np.asarray(x).astype(np.float64)


def striped(idx):
    return np.tile(idx.reshape(-1, 16).T, (8, 1))


CE, CD, D, H1, H2, H3, C, S, N = 640, 128, 768, 1024, 512, 256, 1024, 4096, 1024
EPS, BC = 1e-5, 0.25


def norm(v):
    mu = v.mean(axis=1, keepdims=True)
    var = ((v - mu) ** 2).mean(axis=1, keepdims=True)
    return (v - mu) / np.sqrt(var + EPS)


def setup_inputs():
    return {
        "base": f32(np.random.standard_normal((C, S))),
        "emb": f32(np.random.standard_normal((CE, N))),
        "dense": f32(np.random.standard_normal((CD, N))),
        "wc": bf(np.random.standard_normal((D, 1)) / np.sqrt(D)),
        "gain0": f32(1.0 + 0.2 * np.random.standard_normal((D, 1))),
        "w1": bf(np.random.standard_normal((D, H1)) / np.sqrt(D)),
        "gain1": f32(1.0 + 0.2 * np.random.standard_normal((H1, 1))),
        "w2": bf(np.random.standard_normal((H1, H2)) / np.sqrt(H1)),
        "gain2": f32(1.0 + 0.2 * np.random.standard_normal((H2, 1))),
        "w3": bf(np.random.standard_normal((H2, H3)) / np.sqrt(H2)),
        "gain3": f32(1.0 + 0.2 * np.random.standard_normal((H3, 1))),
        "shift3": f32(0.2 * np.random.standard_normal((H3, 1))),
        "offs": striped(np.random.permutation(S)[:N]),
    }


def reference(base, emb, dense, wc, gain0, w1, gain1, w2, gain2, w3, gain3, shift3, offs):
    idx = offs[:16].T.reshape(-1)
    x0 = np.concatenate([f64(emb), f64(dense)], axis=0)
    s = f64(wc).T @ x0
    cross = (x0 * s + BC) + x0
    h = f64(gain0) * norm(x0)
    h = f64(gain1) * norm(f64(w1).T @ h)
    h = f64(gain2) * norm(f64(w2).T @ h)
    h = f64(gain3) * norm(f64(w3).T @ h) + f64(shift3)
    out = f64(base).copy()
    out[:, idx] = np.concatenate([cross, h], axis=0)
    return out

@@ -1,0 +1,165 @@
+import concourse.mybir as mybir
+from concourse.masks import make_identity
+
+F32, BF16, U16 = mybir.dt.float32, mybir.dt.bfloat16, mybir.dt.uint16
+ADD, MULT = mybir.AluOpType.add, mybir.AluOpType.mult
+IDENTITY, SQRT = mybir.ActivationFunctionType.Identity, mybir.ActivationFunctionType.Sqrt
+
+P = 128
+N = 1024
+S = 4096
+BANK = 512
+CE, D, H1, H2, H3 = 640, 768, 1024, 512, 256
+EPS = 1e-5
+BC = 0.25
+
+FLOPS = 2 * N * (D + D * H1 + H1 * H2 + H2 * H3)
+
+ROW_GAIN0, ROW_GAIN1, ROW_GAIN2, ROW_GAIN3, ROW_SHIFT3, ROW_WC = 0, 6, 14, 18, 20, 32
+
+HALVES = (slice(0, BANK), slice(BANK, N))
+
+
+def statistics(nc, small, v):
+    stats = small.tile([P, 2, 6], F32, name="stats")
+    for i, half in enumerate(HALVES):
+        nc.vector.bn_stats(stats[:, i, :], v[:, half])
+    mean_var = small.tile([P, 2], F32, name="mean_var")
+    nc.vector.bn_aggr(mean_var[:], stats[:].rearrange("p a b -> p (a b)"))
+    return mean_var
+
+
+def coefficients(nc, small, mean_var, gain, eps):
+    std = small.tile([P, 1], F32, name="std")
+    nc.scalar.activation(std[:], mean_var[:, 1:2], SQRT, bias=eps[:])
+    rstd = small.tile([P, 1], F32, name="rstd")
+    nc.vector.reciprocal(rstd[:], std[:])
+    scale = small.tile([P, 1], F32, name="scale")
+    nc.vector.tensor_mul(scale[:], rstd[:], gain)
+    bias = small.tile([P, 1], F32, name="bias")
+    nc.vector.tensor_scalar(bias[:], mean_var[:, 0:1], scale[:], -1.0, MULT, MULT)
+    return scale, bias
+
+
+def linear(nc, psum, weights, acts, m):
+    z = psum.tile([P, N], F32, name="z")
+    last = len(acts) - 1
+    for half in HALVES:
+        for k, act in enumerate(acts):
+            nc.tensor.matmul(
+                z[:, half], weights[k][:, m * P : (m + 1) * P], act[:, half], start=(k == 0), stop=(k == last)
+            )
+    return z
+
+
+def tile_dcn_b_kernel(
+    tc, base, emb, dense, wc, gain0, w1, gain1, w2, gain2, w3, gain3, shift3, offs, out
+):
+    nc = tc.nc
+    with (
+        tc.tile_pool(name="held", bufs=1) as held,
+        tc.tile_pool(name="windows", bufs=6) as windows,
+        tc.tile_pool(name="work", bufs=2) as work,
+        tc.tile_pool(name="small", bufs=4) as small,
+        tc.psum_pool(name="psum", bufs=4) as psum,
+    ):
+        offsets = held.tile([P, N // 16], U16, name="offsets")
+        nc.sync.dma_start(offsets[:], offs)
+
+        x0 = [held.tile([P, N], F32, name=f"x0_{k}") for k in range(D // P)]
+        for k, tile in enumerate(x0):
+            rows = emb[k * P : (k + 1) * P, :] if k < CE // P else dense[k * P - CE : (k + 1) * P - CE, :]
+            nc.sync.dma_start(tile[:], rows)
+
+        staged = held.tile([P, P], F32, name="staged")
+        nc.vector.memset(staged[:], 0.0)
+        for row, vector in (
+            (ROW_GAIN0, gain0),
+            (ROW_GAIN1, gain1),
+            (ROW_GAIN2, gain2),
+            (ROW_GAIN3, gain3),
+            (ROW_SHIFT3, shift3),
+        ):
+            as_rows = vector.rearrange("(r p) o -> r (p o)", p=P)
+            nc.sync.dma_start(staged[row : row + as_rows.shape[0], :], as_rows)
+        wc_rows = held.tile([P, P], BF16, name="wc_rows")
+        nc.sync.dma_start(wc_rows[ROW_WC : ROW_WC + D // P, :], wc.rearrange("(r p) o -> r (p o)", p=P))
+        nc.vector.tensor_copy(staged[ROW_WC : ROW_WC + D // P, :], wc_rows[ROW_WC : ROW_WC + D // P, :])
+
+        w1_sb = [held.tile([P, H1], BF16, name=f"w1_{k}") for k in range(D // P)]
+        w2_sb = [held.tile([P, H2], BF16, name=f"w2_{k}") for k in range(H1 // P)]
+        w3_sb = [held.tile([P, H3], BF16, name=f"w3_{k}") for k in range(H2 // P)]
+        for tiles, weight in ((w1_sb, w1), (w2_sb, w2), (w3_sb, w3)):
+            for k, tile in enumerate(tiles):
+                nc.sync.dma_start(tile[:], weight[k * P : (k + 1) * P, :])
+
+        identity = held.tile([P, P], F32, name="identity")
+        make_identity(nc, identity[:])
+        cols_ps = psum.tile([P, P], F32, name="cols_ps", tag="z")
+        nc.tensor.transpose(cols_ps[:], staged[:], identity[:])
+        cols = held.tile([P, P], F32, name="cols")
+        nc.vector.tensor_copy(cols[:], cols_ps[:])
+
+        eps = held.tile([P, 1], F32, name="eps")
+        nc.vector.memset(eps[:], EPS)
+        quarter = held.tile([P, 1], F32, name="quarter")
+        nc.vector.memset(quarter[:], BC)
+
+        wc_wide = held.tile([P, D // P, P], BF16, name="wc_wide")
+        nc.vector.tensor_copy(
+            wc_wide[:], cols[:, ROW_WC : ROW_WC + D // P].unsqueeze(2).to_broadcast([P, D // P, P])
+        )
+
+        shift_wide = [held.tile([P, N], F32, name=f"shift_wide_{m}") for m in range(H3 // P)]
+        for m, tile in enumerate(shift_wide):
+            nc.gpsimd.tensor_copy(tile[:], cols[:, ROW_SHIFT3 + m : ROW_SHIFT3 + m + 1].to_broadcast([P, N]))
+
+        x0_bf = [held.tile([P, N], BF16, name=f"x0_bf_{k}") for k in range(D // P)]
+        h0 = [held.tile([P, N], BF16, name=f"h0_{k}") for k in range(D // P)]
+        for k in range(D // P):
+            nc.vector.tensor_copy(x0_bf[k][:], x0[k][:])
+            mean_var = statistics(nc, small, x0[k])
+            scale, bias = coefficients(nc, small, mean_var, cols[:, ROW_GAIN0 + k : ROW_GAIN0 + k + 1], eps)
+            nc.scalar.activation(h0[k][:], x0[k][:], IDENTITY, scale=scale[:], bias=bias[:])
+
+        s_ps = psum.tile([P, N], F32, name="s_ps", tag="z")
+        for half in HALVES:
+            for k in range(D // P):
+                nc.tensor.matmul(
+                    s_ps[:, half], wc_wide[:, k, :], x0_bf[k][:, half], start=(k == 0), stop=(k == D // P - 1)
+                )
+        s = held.tile([P, N], F32, name="s")
+        for half in HALVES:
+            nc.scalar.copy(s[:, half], s_ps[:, half])
+
+        for c in range(D // P):
+            window = windows.tile([P, S], F32, name="window")
+            nc.sync.dma_start(window[:], base[c * P : (c + 1) * P, :])
+            product = work.tile([P, N], F32, name="product")
+            nc.vector.tensor_mul(product[:], x0[c][:], s[:])
+            shifted = work.tile([P, N], F32, name="shifted")
+            nc.scalar.activation(shifted[:], product[:], IDENTITY, bias=quarter[:])
+            nc.vector.tensor_tensor(window[:].indirect(offsets[:]), shifted[:], x0[c][:], ADD)
+            nc.sync.dma_start(out[c * P : (c + 1) * P, :], window[:])
+
+        h1 = [held.tile([P, N], BF16, name=f"h1_{m}") for m in range(H1 // P)]
+        h2 = [held.tile([P, N], BF16, name=f"h2_{m}") for m in range(H2 // P)]
+        for weights, acts, outs, row_gain in ((w1_sb, h0, h1, ROW_GAIN1), (w2_sb, h1, h2, ROW_GAIN2)):
+            for m, h in enumerate(outs):
+                z = linear(nc, psum, weights, acts, m)
+                mean_var = statistics(nc, small, z)
+                scale, bias = coefficients(nc, small, mean_var, cols[:, row_gain + m : row_gain + m + 1], eps)
+                for half in HALVES:
+                    nc.scalar.activation(h[:, half], z[:, half], IDENTITY, scale=scale[:], bias=bias[:])
+
+        for m in range(H3 // P):
+            window = windows.tile([P, S], F32, name="window")
+            nc.sync.dma_start(window[:], base[D + m * P : D + (m + 1) * P, :])
+            z = linear(nc, psum, w3_sb, h2, m)
+            mean_var = statistics(nc, small, z)
+            scale, bias = coefficients(nc, small, mean_var, cols[:, ROW_GAIN3 + m : ROW_GAIN3 + m + 1], eps)
+            scaled = work.tile([P, N], F32, name="scaled")
+            for half in HALVES:
+                nc.scalar.activation(scaled[:, half], z[:, half], IDENTITY, scale=scale[:], bias=bias[:])
+            nc.vector.tensor_tensor(window[:].indirect(offsets[:]), scaled[:], shift_wide[m][:], ADD)
+            nc.sync.dma_start(out[D + m * P : D + (m + 1) * P, :], window[:])

@@ -3,7 +3,9 @@ from concourse.masks import make_identity
 
 F32, BF16, U16 = mybir.dt.float32, mybir.dt.bfloat16, mybir.dt.uint16
 ADD, MULT = mybir.AluOpType.add, mybir.AluOpType.mult
-IDENTITY, SQRT = mybir.ActivationFunctionType.Identity, mybir.ActivationFunctionType.Sqrt
+IDENTITY = mybir.ActivationFunctionType.Identity
+SQUARE = mybir.ActivationFunctionType.Square
+ABS_RSQRT = mybir.ActivationFunctionType.Abs_reciprocal_sqrt
 
 P = 128
 N = 1024
@@ -12,33 +14,13 @@ BANK = 512
 CE, D, H1, H2, H3 = 640, 768, 1024, 512, 256
 EPS = 1e-5
 BC = 0.25
+AHEAD = 2
 
 FLOPS = 2 * N * (D + D * H1 + H1 * H2 + H2 * H3)
 
 ROW_GAIN0, ROW_GAIN1, ROW_GAIN2, ROW_GAIN3, ROW_SHIFT3, ROW_WC = 0, 6, 14, 18, 20, 32
 
 HALVES = (slice(0, BANK), slice(BANK, N))
-
-
-def statistics(nc, small, v):
-    stats = small.tile([P, 2, 6], F32, name="stats")
-    for i, half in enumerate(HALVES):
-        nc.vector.bn_stats(stats[:, i, :], v[:, half])
-    mean_var = small.tile([P, 2], F32, name="mean_var")
-    nc.vector.bn_aggr(mean_var[:], stats[:].rearrange("p a b -> p (a b)"))
-    return mean_var
-
-
-def coefficients(nc, small, mean_var, gain, eps):
-    std = small.tile([P, 1], F32, name="std")
-    nc.scalar.activation(std[:], mean_var[:, 1:2], SQRT, bias=eps[:])
-    rstd = small.tile([P, 1], F32, name="rstd")
-    nc.vector.reciprocal(rstd[:], std[:])
-    scale = small.tile([P, 1], F32, name="scale")
-    nc.vector.tensor_mul(scale[:], rstd[:], gain)
-    bias = small.tile([P, 1], F32, name="bias")
-    nc.vector.tensor_scalar(bias[:], mean_var[:, 0:1], scale[:], -1.0, MULT, MULT)
-    return scale, bias
 
 
 def linear(nc, psum, weights, acts, m):
@@ -52,24 +34,38 @@ def linear(nc, psum, weights, acts, m):
     return z
 
 
+def moments(nc, work, small, z, gain, eps):
+    z_sb = work.tile([P, N], F32, name="z_sb", bufs=4)
+    sums = small.tile([P, 2], F32, name="sums")
+    for i, half in enumerate(HALVES):
+        nc.scalar.activation(z_sb[:, half], z[:, half], IDENTITY, accum_out=sums[:, i : i + 1])
+    neg_mean = small.tile([P, 1], F32, name="neg_mean")
+    neg_parts = small.tile([P, 2], F32, name="neg_parts")
+    nc.scalar.activation(neg_parts[:], sums[:], IDENTITY, scale=-1.0 / N, accum_out=neg_mean[:])
+    squares = work.tile([P, N], BF16, name="squares", bufs=2)
+    sum_squares = small.tile([P, 1], F32, name="sum_squares")
+    nc.scalar.activation(squares[:], z_sb[:], SQUARE, bias=neg_mean[:], accum_out=sum_squares[:])
+    rstd = small.tile([P, 1], F32, name="rstd")
+    nc.scalar.activation(rstd[:], sum_squares[:], ABS_RSQRT, scale=1.0 / N, bias=eps[:])
+    scale = small.tile([P, 1], F32, name="scale")
+    nc.scalar.activation(scale[:], rstd[:], IDENTITY, scale=gain)
+    return z_sb, neg_mean, scale
+
+
 def tile_dcn_b_kernel(
     tc, base, emb, dense, wc, gain0, w1, gain1, w2, gain2, w3, gain3, shift3, offs, out
 ):
     nc = tc.nc
     with (
         tc.tile_pool(name="held", bufs=1) as held,
+        tc.tile_pool(name="acts", bufs=D // P) as acts,
         tc.tile_pool(name="windows", bufs=6) as windows,
         tc.tile_pool(name="work", bufs=2) as work,
-        tc.tile_pool(name="small", bufs=4) as small,
+        tc.tile_pool(name="small", bufs=6) as small,
         tc.psum_pool(name="psum", bufs=4) as psum,
     ):
         offsets = held.tile([P, N // 16], U16, name="offsets")
         nc.sync.dma_start(offsets[:], offs)
-
-        x0 = [held.tile([P, N], F32, name=f"x0_{k}") for k in range(D // P)]
-        for k, tile in enumerate(x0):
-            rows = emb[k * P : (k + 1) * P, :] if k < CE // P else dense[k * P - CE : (k + 1) * P - CE, :]
-            nc.sync.dma_start(tile[:], rows)
 
         staged = held.tile([P, P], F32, name="staged")
         nc.vector.memset(staged[:], 0.0)
@@ -81,17 +77,36 @@ def tile_dcn_b_kernel(
             (ROW_SHIFT3, shift3),
         ):
             as_rows = vector.rearrange("(r p) o -> r (p o)", p=P)
-            nc.sync.dma_start(staged[row : row + as_rows.shape[0], :], as_rows)
+            nc.scalar.dma_start(staged[row : row + as_rows.shape[0], :], as_rows)
         wc_rows = held.tile([P, P], BF16, name="wc_rows")
-        nc.sync.dma_start(wc_rows[ROW_WC : ROW_WC + D // P, :], wc.rearrange("(r p) o -> r (p o)", p=P))
+        nc.scalar.dma_start(wc_rows[ROW_WC : ROW_WC + D // P, :], wc.rearrange("(r p) o -> r (p o)", p=P))
         nc.vector.tensor_copy(staged[ROW_WC : ROW_WC + D // P, :], wc_rows[ROW_WC : ROW_WC + D // P, :])
 
-        w1_sb = [held.tile([P, H1], BF16, name=f"w1_{k}") for k in range(D // P)]
-        w2_sb = [held.tile([P, H2], BF16, name=f"w2_{k}") for k in range(H1 // P)]
-        w3_sb = [held.tile([P, H3], BF16, name=f"w3_{k}") for k in range(H2 // P)]
-        for tiles, weight in ((w1_sb, w1), (w2_sb, w2), (w3_sb, w3)):
-            for k, tile in enumerate(tiles):
-                nc.sync.dma_start(tile[:], weight[k * P : (k + 1) * P, :])
+        x0 = [held.tile([P, N], F32, name=f"x0_{k}") for k in range(D // P)]
+        for k in range(D // P):
+            rows = emb[k * P : (k + 1) * P, :] if k < CE // P else dense[k * P - CE : (k + 1) * P - CE, :]
+            nc.sync.dma_start(x0[k][:], rows)
+
+        w1_all = held.tile([P, D // P, H1], BF16, name="w1_all")
+        w2_all = held.tile([P, H1 // P, H2], BF16, name="w2_all")
+        w3_all = held.tile([P, H2 // P, H3], BF16, name="w3_all")
+        w1_rows = w1.rearrange("(k p) h -> p k h", p=P)
+        weight_loads = (
+            (w1_all[:, :, : H1 // 2], w1_rows[:, :, : H1 // 2]),
+            (w1_all[:, :, H1 // 2 :], w1_rows[:, :, H1 // 2 :]),
+            (w2_all[:], w2.rearrange("(k p) h -> p k h", p=P)),
+            (w3_all[:], w3.rearrange("(k p) h -> p k h", p=P)),
+        )
+        cross_windows = []
+        for c in range(D // P):
+            if c < len(weight_loads):
+                nc.sync.dma_start(weight_loads[c][0], weight_loads[c][1])
+            window = windows.tile([P, S], F32, name="window")
+            nc.sync.dma_start(window[:], base[c * P : (c + 1) * P, :])
+            cross_windows.append(window)
+        w1_sb = [w1_all[:, k, :] for k in range(D // P)]
+        w2_sb = [w2_all[:, k, :] for k in range(H1 // P)]
+        w3_sb = [w3_all[:, k, :] for k in range(H2 // P)]
 
         identity = held.tile([P, P], F32, name="identity")
         make_identity(nc, identity[:])
@@ -110,56 +125,68 @@ def tile_dcn_b_kernel(
             wc_wide[:], cols[:, ROW_WC : ROW_WC + D // P].unsqueeze(2).to_broadcast([P, D // P, P])
         )
 
-        shift_wide = [held.tile([P, N], F32, name=f"shift_wide_{m}") for m in range(H3 // P)]
-        for m, tile in enumerate(shift_wide):
-            nc.gpsimd.tensor_copy(tile[:], cols[:, ROW_SHIFT3 + m : ROW_SHIFT3 + m + 1].to_broadcast([P, N]))
-
-        x0_bf = [held.tile([P, N], BF16, name=f"x0_bf_{k}") for k in range(D // P)]
-        h0 = [held.tile([P, N], BF16, name=f"h0_{k}") for k in range(D // P)]
+        h0 = [acts.tile([P, N], BF16, name=f"h0_{k}", tag="h0_then_h2") for k in range(D // P)]
+        s_ps = psum.tile([P, N], F32, name="s_ps", tag="z")
         for k in range(D // P):
-            nc.vector.tensor_copy(x0_bf[k][:], x0[k][:])
-            mean_var = statistics(nc, small, x0[k])
-            scale, bias = coefficients(nc, small, mean_var, cols[:, ROW_GAIN0 + k : ROW_GAIN0 + k + 1], eps)
+            stats = small.tile([P, 2, 6], F32, name="stats")
+            for i, half in enumerate(HALVES):
+                nc.vector.bn_stats(stats[:, i, :], x0[k][:, half])
+            mean_var = small.tile([P, 2], F32, name="mean_var")
+            nc.vector.bn_aggr(mean_var[:], stats[:].rearrange("p a b -> p (a b)"))
+            rstd = small.tile([P, 1], F32, name="rstd0")
+            nc.scalar.activation(rstd[:], mean_var[:, 1:2], ABS_RSQRT, bias=eps[:])
+            scale = small.tile([P, 1], F32, name="scale0")
+            nc.vector.tensor_scalar_mul(scale[:], rstd[:], cols[:, ROW_GAIN0 + k : ROW_GAIN0 + k + 1])
+            bias = small.tile([P, 1], F32, name="bias0")
+            nc.vector.tensor_scalar(bias[:], mean_var[:, 0:1], scale[:], -1.0, MULT, MULT)
             nc.scalar.activation(h0[k][:], x0[k][:], IDENTITY, scale=scale[:], bias=bias[:])
 
-        s_ps = psum.tile([P, N], F32, name="s_ps", tag="z")
-        for half in HALVES:
-            for k in range(D // P):
+            x0_bf = work.tile([P, N], BF16, name="x0_bf")
+            nc.gpsimd.tensor_copy(x0_bf[:], x0[k][:])
+            for half in HALVES:
                 nc.tensor.matmul(
-                    s_ps[:, half], wc_wide[:, k, :], x0_bf[k][:, half], start=(k == 0), stop=(k == D // P - 1)
+                    s_ps[:, half], wc_wide[:, k, :], x0_bf[:, half], start=(k == 0), stop=(k == D // P - 1)
                 )
         s = held.tile([P, N], F32, name="s")
         for half in HALVES:
             nc.scalar.copy(s[:, half], s_ps[:, half])
 
-        for c in range(D // P):
-            window = windows.tile([P, S], F32, name="window")
-            nc.sync.dma_start(window[:], base[c * P : (c + 1) * P, :])
-            product = work.tile([P, N], F32, name="product")
-            nc.vector.tensor_mul(product[:], x0[c][:], s[:])
-            shifted = work.tile([P, N], F32, name="shifted")
-            nc.scalar.activation(shifted[:], product[:], IDENTITY, bias=quarter[:])
-            nc.vector.tensor_tensor(window[:].indirect(offsets[:]), shifted[:], x0[c][:], ADD)
-            nc.sync.dma_start(out[c * P : (c + 1) * P, :], window[:])
+        shift_wide = [held.tile([P, N], F32, name=f"shift_wide_{m}") for m in range(H3 // P)]
+        for m, tile in enumerate(shift_wide):
+            nc.gpsimd.tensor_copy(tile[:], cols[:, ROW_SHIFT3 + m : ROW_SHIFT3 + m + 1].to_broadcast([P, N]))
+
+        def cross_term(c):
+            term = work.tile([P, N], F32, name="term", bufs=AHEAD + 1)
+            nc.vector.tensor_mul(term[:], x0[c][:], s[:])
+            nc.scalar.activation(term[:], term[:], IDENTITY, bias=quarter[:])
+            return term
+
+        terms = [cross_term(c) for c in range(AHEAD)]
 
         h1 = [held.tile([P, N], BF16, name=f"h1_{m}") for m in range(H1 // P)]
-        h2 = [held.tile([P, N], BF16, name=f"h2_{m}") for m in range(H2 // P)]
-        for weights, acts, outs, row_gain in ((w1_sb, h0, h1, ROW_GAIN1), (w2_sb, h1, h2, ROW_GAIN2)):
-            for m, h in enumerate(outs):
-                z = linear(nc, psum, weights, acts, m)
-                mean_var = statistics(nc, small, z)
-                scale, bias = coefficients(nc, small, mean_var, cols[:, row_gain + m : row_gain + m + 1], eps)
-                for half in HALVES:
-                    nc.scalar.activation(h[:, half], z[:, half], IDENTITY, scale=scale[:], bias=bias[:])
+        for m, h in enumerate(h1):
+            z = linear(nc, psum, w1_sb, h0, m)
+            z_sb, neg_mean, scale = moments(nc, work, small, z, cols[:, ROW_GAIN1 + m : ROW_GAIN1 + m + 1], eps)
+            nc.vector.tensor_scalar(h[:], z_sb[:], neg_mean[:], scale[:], ADD, MULT)
+
+        h2 = [acts.tile([P, N], BF16, name=f"h2_{m}", tag="h0_then_h2") for m in range(H2 // P)]
+        scaled = [held.tile([P, N], F32, name=f"scaled_{m}") for m in range(H3 // P)]
+        for weights, inputs, outputs, row_gain in ((w2_sb, h1, h2, ROW_GAIN2), (w3_sb, h2, scaled, ROW_GAIN3)):
+            for m, h in enumerate(outputs):
+                z = linear(nc, psum, weights, inputs, m)
+                z_sb, neg_mean, scale = moments(nc, work, small, z, cols[:, row_gain + m : row_gain + m + 1], eps)
+                bias = small.tile([P, 1], F32, name="bias")
+                nc.scalar.activation(bias[:], neg_mean[:], IDENTITY, scale=scale[:])
+                nc.scalar.activation(h[:], z_sb[:], IDENTITY, scale=scale[:], bias=bias[:])
+
+        for c, window in enumerate(cross_windows):
+            if c + AHEAD < D // P:
+                terms.append(cross_term(c + AHEAD))
+            nc.vector.tensor_tensor(window[:].indirect(offsets[:]), terms[c][:], x0[c][:], ADD)
+            nc.sync.dma_start(out[c * P : (c + 1) * P, :], window[:])
 
         for m in range(H3 // P):
             window = windows.tile([P, S], F32, name="window")
             nc.sync.dma_start(window[:], base[D + m * P : D + (m + 1) * P, :])
-            z = linear(nc, psum, w3_sb, h2, m)
-            mean_var = statistics(nc, small, z)
-            scale, bias = coefficients(nc, small, mean_var, cols[:, ROW_GAIN3 + m : ROW_GAIN3 + m + 1], eps)
-            scaled = work.tile([P, N], F32, name="scaled")
-            for half in HALVES:
-                nc.scalar.activation(scaled[:, half], z[:, half], IDENTITY, scale=scale[:], bias=bias[:])
-            nc.vector.tensor_tensor(window[:].indirect(offsets[:]), scaled[:], shift_wide[m][:], ADD)
+            nc.vector.tensor_tensor(window[:].indirect(offsets[:]), scaled[m][:], shift_wide[m][:], ADD)
             nc.sync.dma_start(out[D + m * P : D + (m + 1) * P, :], window[:])

@@ -2,7 +2,7 @@ import concourse.mybir as mybir
 from concourse.masks import make_identity
 
 F32, BF16, U16 = mybir.dt.float32, mybir.dt.bfloat16, mybir.dt.uint16
-ADD, MULT = mybir.AluOpType.add, mybir.AluOpType.mult
+ADD, SUBTRACT, MULT = mybir.AluOpType.add, mybir.AluOpType.subtract, mybir.AluOpType.mult
 IDENTITY = mybir.ActivationFunctionType.Identity
 SQUARE = mybir.ActivationFunctionType.Square
 ABS_RSQRT = mybir.ActivationFunctionType.Abs_reciprocal_sqrt
@@ -14,7 +14,6 @@ BANK = 512
 CE, D, H1, H2, H3 = 640, 768, 1024, 512, 256
 EPS = 1e-5
 BC = 0.25
-AHEAD = 2
 
 FLOPS = 2 * N * (D + D * H1 + H1 * H2 + H2 * H3)
 
@@ -26,16 +25,29 @@ HALVES = (slice(0, BANK), slice(BANK, N))
 def linear(nc, psum, weights, acts, m):
     z = psum.tile([P, N], F32, name="z")
     last = len(acts) - 1
-    for half in HALVES:
-        for k, act in enumerate(acts):
+    for k, act in enumerate(acts):
+        for half in HALVES:
             nc.tensor.matmul(
                 z[:, half], weights[k][:, m * P : (m + 1) * P], act[:, half], start=(k == 0), stop=(k == last)
             )
     return z
 
 
-def moments(nc, work, small, z, gain, eps):
-    z_sb = work.tile([P, N], F32, name="z_sb", bufs=4)
+def vector_moments(nc, small, v, gain, eps):
+    stats = small.tile([P, 2, 6], F32, name="stats")
+    for i, half in enumerate(HALVES):
+        nc.vector.bn_stats(stats[:, i, :], v[:, half])
+    mean_var = small.tile([P, 2], F32, name="mean_var")
+    nc.vector.bn_aggr(mean_var[:], stats[:].rearrange("p a b -> p (a b)"))
+    rstd = small.tile([P, 1], F32, name="rstd_v")
+    nc.scalar.activation(rstd[:], mean_var[:, 1:2], ABS_RSQRT, bias=eps[:])
+    scale = small.tile([P, 1], F32, name="scale_v")
+    nc.vector.tensor_scalar_mul(scale[:], rstd[:], gain)
+    return mean_var, scale
+
+
+def normalise(nc, work, small, z, gain, eps, h):
+    z_sb = work.tile([P, N], F32, name="z_sb", bufs=3)
     sums = small.tile([P, 2], F32, name="sums")
     for i, half in enumerate(HALVES):
         nc.scalar.activation(z_sb[:, half], z[:, half], IDENTITY, accum_out=sums[:, i : i + 1])
@@ -49,7 +61,10 @@ def moments(nc, work, small, z, gain, eps):
     nc.scalar.activation(rstd[:], sum_squares[:], ABS_RSQRT, scale=1.0 / N, bias=eps[:])
     scale = small.tile([P, 1], F32, name="scale")
     nc.scalar.activation(scale[:], rstd[:], IDENTITY, scale=gain)
-    return z_sb, neg_mean, scale
+    bias = small.tile([P, 1], F32, name="bias")
+    nc.scalar.activation(bias[:], neg_mean[:], IDENTITY, scale=scale[:])
+    for half in HALVES:
+        nc.scalar.activation(h[:, half], z_sb[:, half], IDENTITY, scale=scale[:], bias=bias[:])
 
 
 def tile_dcn_b_kernel(
@@ -62,10 +77,17 @@ def tile_dcn_b_kernel(
         tc.tile_pool(name="windows", bufs=6) as windows,
         tc.tile_pool(name="work", bufs=2) as work,
         tc.tile_pool(name="small", bufs=6) as small,
-        tc.psum_pool(name="psum", bufs=4) as psum,
+        tc.psum_pool(name="psum", bufs=3) as psum,
+        tc.psum_pool(name="psum_s", bufs=1) as psum_s,
     ):
         offsets = held.tile([P, N // 16], U16, name="offsets")
         nc.sync.dma_start(offsets[:], offs)
+
+        x0 = [held.tile([P, N], F32, name=f"x0_{k}") for k in range(D // P)]
+        x0_rows = [emb[k * P : (k + 1) * P, :] for k in range(CE // P)] + [dense]
+        w1_all = held.tile([P, D // P, H1], BF16, name="w1_all")
+        nc.sync.dma_start(x0[0][:], x0_rows[0])
+        nc.sync.dma_start(w1_all[:, 0, : H1 // 2], w1[0:P, : H1 // 2])
 
         staged = held.tile([P, P], F32, name="staged")
         nc.vector.memset(staged[:], 0.0)
@@ -77,33 +99,29 @@ def tile_dcn_b_kernel(
             (ROW_SHIFT3, shift3),
         ):
             as_rows = vector.rearrange("(r p) o -> r (p o)", p=P)
-            nc.scalar.dma_start(staged[row : row + as_rows.shape[0], :], as_rows)
+            nc.sync.dma_start(staged[row : row + as_rows.shape[0], :], as_rows)
         wc_rows = held.tile([P, P], BF16, name="wc_rows")
-        nc.scalar.dma_start(wc_rows[ROW_WC : ROW_WC + D // P, :], wc.rearrange("(r p) o -> r (p o)", p=P))
+        nc.sync.dma_start(wc_rows[ROW_WC : ROW_WC + D // P, :], wc.rearrange("(r p) o -> r (p o)", p=P))
         nc.vector.tensor_copy(staged[ROW_WC : ROW_WC + D // P, :], wc_rows[ROW_WC : ROW_WC + D // P, :])
 
-        x0 = [held.tile([P, N], F32, name=f"x0_{k}") for k in range(D // P)]
-        for k in range(D // P):
-            rows = emb[k * P : (k + 1) * P, :] if k < CE // P else dense[k * P - CE : (k + 1) * P - CE, :]
-            nc.sync.dma_start(x0[k][:], rows)
+        for k in range(1, D // P):
+            nc.sync.dma_start(x0[k][:], x0_rows[k])
+            nc.sync.dma_start(w1_all[:, k, : H1 // 2], w1[k * P : (k + 1) * P, : H1 // 2])
 
-        w1_all = held.tile([P, D // P, H1], BF16, name="w1_all")
         w2_all = held.tile([P, H1 // P, H2], BF16, name="w2_all")
         w3_all = held.tile([P, H2 // P, H3], BF16, name="w3_all")
-        w1_rows = w1.rearrange("(k p) h -> p k h", p=P)
-        weight_loads = (
-            (w1_all[:, :, : H1 // 2], w1_rows[:, :, : H1 // 2]),
-            (w1_all[:, :, H1 // 2 :], w1_rows[:, :, H1 // 2 :]),
+        later_weights = (
+            (w1_all[:, :, H1 // 2 :], w1.rearrange("(k p) h -> p k h", p=P)[:, :, H1 // 2 :]),
             (w2_all[:], w2.rearrange("(k p) h -> p k h", p=P)),
             (w3_all[:], w3.rearrange("(k p) h -> p k h", p=P)),
         )
         cross_windows = []
         for c in range(D // P):
-            if c < len(weight_loads):
-                nc.sync.dma_start(weight_loads[c][0], weight_loads[c][1])
             window = windows.tile([P, S], F32, name="window")
             nc.sync.dma_start(window[:], base[c * P : (c + 1) * P, :])
             cross_windows.append(window)
+            if c < len(later_weights):
+                nc.sync.dma_start(later_weights[c][0], later_weights[c][1])
         w1_sb = [w1_all[:, k, :] for k in range(D // P)]
         w2_sb = [w2_all[:, k, :] for k in range(H1 // P)]
         w3_sb = [w3_all[:, k, :] for k in range(H2 // P)]
@@ -117,8 +135,6 @@ def tile_dcn_b_kernel(
 
         eps = held.tile([P, 1], F32, name="eps")
         nc.vector.memset(eps[:], EPS)
-        quarter = held.tile([P, 1], F32, name="quarter")
-        nc.vector.memset(quarter[:], BC)
 
         wc_wide = held.tile([P, D // P, P], BF16, name="wc_wide")
         nc.vector.tensor_copy(
@@ -126,17 +142,9 @@ def tile_dcn_b_kernel(
         )
 
         h0 = [acts.tile([P, N], BF16, name=f"h0_{k}", tag="h0_then_h2") for k in range(D // P)]
-        s_ps = psum.tile([P, N], F32, name="s_ps", tag="z")
+        s_ps = psum_s.tile([P, N], F32, name="s_ps")
         for k in range(D // P):
-            stats = small.tile([P, 2, 6], F32, name="stats")
-            for i, half in enumerate(HALVES):
-                nc.vector.bn_stats(stats[:, i, :], x0[k][:, half])
-            mean_var = small.tile([P, 2], F32, name="mean_var")
-            nc.vector.bn_aggr(mean_var[:], stats[:].rearrange("p a b -> p (a b)"))
-            rstd = small.tile([P, 1], F32, name="rstd0")
-            nc.scalar.activation(rstd[:], mean_var[:, 1:2], ABS_RSQRT, bias=eps[:])
-            scale = small.tile([P, 1], F32, name="scale0")
-            nc.vector.tensor_scalar_mul(scale[:], rstd[:], cols[:, ROW_GAIN0 + k : ROW_GAIN0 + k + 1])
+            mean_var, scale = vector_moments(nc, small, x0[k], cols[:, ROW_GAIN0 + k : ROW_GAIN0 + k + 1], eps)
             bias = small.tile([P, 1], F32, name="bias0")
             nc.vector.tensor_scalar(bias[:], mean_var[:, 0:1], scale[:], -1.0, MULT, MULT)
             nc.scalar.activation(h0[k][:], x0[k][:], IDENTITY, scale=scale[:], bias=bias[:])
@@ -147,46 +155,38 @@ def tile_dcn_b_kernel(
                 nc.tensor.matmul(
                     s_ps[:, half], wc_wide[:, k, :], x0_bf[:, half], start=(k == 0), stop=(k == D // P - 1)
                 )
-        s = held.tile([P, N], F32, name="s")
-        for half in HALVES:
-            nc.scalar.copy(s[:, half], s_ps[:, half])
 
         shift_wide = [held.tile([P, N], F32, name=f"shift_wide_{m}") for m in range(H3 // P)]
         for m, tile in enumerate(shift_wide):
             nc.gpsimd.tensor_copy(tile[:], cols[:, ROW_SHIFT3 + m : ROW_SHIFT3 + m + 1].to_broadcast([P, N]))
 
-        def cross_term(c):
-            term = work.tile([P, N], F32, name="term", bufs=AHEAD + 1)
-            nc.vector.tensor_mul(term[:], x0[c][:], s[:])
-            nc.scalar.activation(term[:], term[:], IDENTITY, bias=quarter[:])
-            return term
-
-        terms = [cross_term(c) for c in range(AHEAD)]
-
         h1 = [held.tile([P, N], BF16, name=f"h1_{m}") for m in range(H1 // P)]
-        for m, h in enumerate(h1):
-            z = linear(nc, psum, w1_sb, h0, m)
-            z_sb, neg_mean, scale = moments(nc, work, small, z, cols[:, ROW_GAIN1 + m : ROW_GAIN1 + m + 1], eps)
-            nc.vector.tensor_scalar(h[:], z_sb[:], neg_mean[:], scale[:], ADD, MULT)
-
         h2 = [acts.tile([P, N], BF16, name=f"h2_{m}", tag="h0_then_h2") for m in range(H2 // P)]
-        scaled = [held.tile([P, N], F32, name=f"scaled_{m}") for m in range(H3 // P)]
-        for weights, inputs, outputs, row_gain in ((w2_sb, h1, h2, ROW_GAIN2), (w3_sb, h2, scaled, ROW_GAIN3)):
+        for weights, inputs, outputs, row_gain in ((w1_sb, h0, h1, ROW_GAIN1), (w2_sb, h1, h2, ROW_GAIN2)):
             for m, h in enumerate(outputs):
                 z = linear(nc, psum, weights, inputs, m)
-                z_sb, neg_mean, scale = moments(nc, work, small, z, cols[:, row_gain + m : row_gain + m + 1], eps)
-                bias = small.tile([P, 1], F32, name="bias")
-                nc.scalar.activation(bias[:], neg_mean[:], IDENTITY, scale=scale[:])
-                nc.scalar.activation(h[:], z_sb[:], IDENTITY, scale=scale[:], bias=bias[:])
+                normalise(nc, work, small, z, cols[:, row_gain + m : row_gain + m + 1], eps, h)
 
         for c, window in enumerate(cross_windows):
-            if c + AHEAD < D // P:
-                terms.append(cross_term(c + AHEAD))
-            nc.vector.tensor_tensor(window[:].indirect(offsets[:]), terms[c][:], x0[c][:], ADD)
-            nc.sync.dma_start(out[c * P : (c + 1) * P, :], window[:])
+            product = work.tile([P, N], F32, name="product")
+            for half in HALVES:
+                nc.vector.tensor_mul(product[:, half], x0[c][:, half], s_ps[:, half])
+            term = work.tile([P, N], F32, name="term")
+            nc.vector.tensor_scalar_add(term[:], product[:], BC)
+            nc.vector.tensor_tensor(window[:].indirect(offsets[:]), term[:], x0[c][:], ADD)
+            nc.gpsimd.dma_start(out[c * P : (c + 1) * P, :], window[:])
 
         for m in range(H3 // P):
             window = windows.tile([P, S], F32, name="window")
             nc.sync.dma_start(window[:], base[D + m * P : D + (m + 1) * P, :])
-            nc.vector.tensor_tensor(window[:].indirect(offsets[:]), scaled[m][:], shift_wide[m][:], ADD)
+            gain = cols[:, ROW_GAIN3 + m : ROW_GAIN3 + m + 1]
+            z = linear(nc, psum, w3_sb, h2, m)
+            scaled = work.tile([P, N], F32, name="scaled")
+            if m == 0:
+                mean_var, scale = vector_moments(nc, small, z, gain, eps)
+                for half in HALVES:
+                    nc.vector.tensor_scalar(scaled[:, half], z[:, half], mean_var[:, 0:1], scale[:], SUBTRACT, MULT)
+            else:
+                normalise(nc, work, small, z, gain, eps, scaled)
+            nc.vector.tensor_tensor(window[:].indirect(offsets[:]), scaled[:], shift_wide[m][:], ADD)
             nc.sync.dma_start(out[D + m * P : D + (m + 1) * P, :], window[:])

@@ -12,6 +12,7 @@ N = 1024
 S = 4096
 BANK = 512
 CE, D, H1, H2, H3 = 640, 768, 1024, 512, 256
+C = D + H3
 EPS = 1e-5
 BC = 0.25
 
@@ -47,24 +48,18 @@ def vector_moments(nc, small, v, gain, eps):
 
 
 def normalise(nc, work, small, z, gain, eps, h):
-    z_sb = work.tile([P, N], F32, name="z_sb", bufs=3)
+    squares = work.tile([P, N], BF16, name="squares")
     sums = small.tile([P, 2], F32, name="sums")
     for i, half in enumerate(HALVES):
-        nc.scalar.activation(z_sb[:, half], z[:, half], IDENTITY, accum_out=sums[:, i : i + 1])
-    neg_mean = small.tile([P, 1], F32, name="neg_mean")
-    neg_parts = small.tile([P, 2], F32, name="neg_parts")
-    nc.scalar.activation(neg_parts[:], sums[:], IDENTITY, scale=-1.0 / N, accum_out=neg_mean[:])
-    squares = work.tile([P, N], BF16, name="squares", bufs=2)
-    sum_squares = small.tile([P, 1], F32, name="sum_squares")
-    nc.scalar.activation(squares[:], z_sb[:], SQUARE, bias=neg_mean[:], accum_out=sum_squares[:])
+        nc.scalar.activation(squares[:, half], z[:, half], SQUARE, accum_out=sums[:, i : i + 1])
+    second = small.tile([P, 1], F32, name="second")
+    nc.scalar.activation(second[:], sums[:, 1:2], IDENTITY, scale=1.0 / N, bias=eps[:])
     rstd = small.tile([P, 1], F32, name="rstd")
-    nc.scalar.activation(rstd[:], sum_squares[:], ABS_RSQRT, scale=1.0 / N, bias=eps[:])
+    nc.scalar.activation(rstd[:], sums[:, 0:1], ABS_RSQRT, scale=1.0 / N, bias=second[:])
     scale = small.tile([P, 1], F32, name="scale")
     nc.scalar.activation(scale[:], rstd[:], IDENTITY, scale=gain)
-    bias = small.tile([P, 1], F32, name="bias")
-    nc.scalar.activation(bias[:], neg_mean[:], IDENTITY, scale=scale[:])
     for half in HALVES:
-        nc.scalar.activation(h[:, half], z_sb[:, half], IDENTITY, scale=scale[:], bias=bias[:])
+        nc.scalar.activation(h[:, half], z[:, half], IDENTITY, scale=scale[:])
 
 
 def tile_dcn_b_kernel(
@@ -74,7 +69,7 @@ def tile_dcn_b_kernel(
     with (
         tc.tile_pool(name="held", bufs=1) as held,
         tc.tile_pool(name="acts", bufs=D // P) as acts,
-        tc.tile_pool(name="windows", bufs=6) as windows,
+        tc.tile_pool(name="windows", bufs=C // P) as windows,
         tc.tile_pool(name="work", bufs=2) as work,
         tc.tile_pool(name="small", bufs=6) as small,
         tc.psum_pool(name="psum", bufs=3) as psum,
@@ -115,11 +110,11 @@ def tile_dcn_b_kernel(
             (w2_all[:], w2.rearrange("(k p) h -> p k h", p=P)),
             (w3_all[:], w3.rearrange("(k p) h -> p k h", p=P)),
         )
-        cross_windows = []
-        for c in range(D // P):
+        all_windows = []
+        for c in range(C // P):
             window = windows.tile([P, S], F32, name="window")
             nc.sync.dma_start(window[:], base[c * P : (c + 1) * P, :])
-            cross_windows.append(window)
+            all_windows.append(window)
             if c < len(later_weights):
                 nc.sync.dma_start(later_weights[c][0], later_weights[c][1])
         w1_sb = [w1_all[:, k, :] for k in range(D // P)]
@@ -167,21 +162,18 @@ def tile_dcn_b_kernel(
                 z = linear(nc, psum, weights, inputs, m)
                 normalise(nc, work, small, z, cols[:, row_gain + m : row_gain + m + 1], eps, h)
 
-        for c, window in enumerate(cross_windows):
-            product = work.tile([P, N], F32, name="product")
+        for c, window in enumerate(all_windows[: D // P]):
+            term = work.tile([P, N], F32, name="term", tag="addend", bufs=3)
             for half in HALVES:
-                nc.vector.tensor_mul(product[:, half], x0[c][:, half], s_ps[:, half])
-            term = work.tile([P, N], F32, name="term")
-            nc.vector.tensor_scalar_add(term[:], product[:], BC)
+                nc.vector.tensor_mul(term[:, half], x0[c][:, half], s_ps[:, half])
+            nc.vector.tensor_scalar_add(term[:], term[:], BC)
             nc.vector.tensor_tensor(window[:].indirect(offsets[:]), term[:], x0[c][:], ADD)
-            nc.gpsimd.dma_start(out[c * P : (c + 1) * P, :], window[:])
+            nc.sync.dma_start(out[c * P : (c + 1) * P, :], window[:])
 
-        for m in range(H3 // P):
-            window = windows.tile([P, S], F32, name="window")
-            nc.sync.dma_start(window[:], base[D + m * P : D + (m + 1) * P, :])
+        for m, window in enumerate(all_windows[D // P :]):
             gain = cols[:, ROW_GAIN3 + m : ROW_GAIN3 + m + 1]
             z = linear(nc, psum, w3_sb, h2, m)
-            scaled = work.tile([P, N], F32, name="scaled")
+            scaled = work.tile([P, N], F32, name="scaled", tag="addend", bufs=3)
             if m == 0:
                 mean_var, scale = vector_moments(nc, small, z, gain, eps)
                 for half in HALVES:

@@ -2,7 +2,7 @@ import concourse.mybir as mybir
 from concourse.masks import make_identity
 
 F32, BF16, U16 = mybir.dt.float32, mybir.dt.bfloat16, mybir.dt.uint16
-ADD, SUBTRACT, MULT = mybir.AluOpType.add, mybir.AluOpType.subtract, mybir.AluOpType.mult
+ADD, MULT = mybir.AluOpType.add, mybir.AluOpType.mult
 IDENTITY = mybir.ActivationFunctionType.Identity
 SQUARE = mybir.ActivationFunctionType.Square
 ABS_RSQRT = mybir.ActivationFunctionType.Abs_reciprocal_sqrt
@@ -48,7 +48,7 @@ def vector_moments(nc, small, v, gain, eps):
 
 
 def normalise(nc, work, small, z, gain, eps, h):
-    squares = work.tile([P, N], BF16, name="squares")
+    squares = work.tile([P, N], BF16, name="squares", bufs=1)
     sums = small.tile([P, 2], F32, name="sums")
     for i, half in enumerate(HALVES):
         nc.scalar.activation(squares[:, half], z[:, half], SQUARE, accum_out=sums[:, i : i + 1])
@@ -80,9 +80,7 @@ def tile_dcn_b_kernel(
 
         x0 = [held.tile([P, N], F32, name=f"x0_{k}") for k in range(D // P)]
         x0_rows = [emb[k * P : (k + 1) * P, :] for k in range(CE // P)] + [dense]
-        w1_all = held.tile([P, D // P, H1], BF16, name="w1_all")
         nc.sync.dma_start(x0[0][:], x0_rows[0])
-        nc.sync.dma_start(w1_all[:, 0, : H1 // 2], w1[0:P, : H1 // 2])
 
         staged = held.tile([P, P], F32, name="staged")
         nc.vector.memset(staged[:], 0.0)
@@ -101,10 +99,11 @@ def tile_dcn_b_kernel(
 
         for k in range(1, D // P):
             nc.sync.dma_start(x0[k][:], x0_rows[k])
-            nc.sync.dma_start(w1_all[:, k, : H1 // 2], w1[k * P : (k + 1) * P, : H1 // 2])
 
+        w1_all = held.tile([P, D // P, H1], BF16, name="w1_all")
         w2_all = held.tile([P, H1 // P, H2], BF16, name="w2_all")
         w3_all = held.tile([P, H2 // P, H3], BF16, name="w3_all")
+        nc.sync.dma_start(w1_all[:, :, : H1 // 2], w1.rearrange("(k p) h -> p k h", p=P)[:, :, : H1 // 2])
         later_weights = (
             (w1_all[:, :, H1 // 2 :], w1.rearrange("(k p) h -> p k h", p=P)[:, :, H1 // 2 :]),
             (w2_all[:], w2.rearrange("(k p) h -> p k h", p=P)),
@@ -163,7 +162,7 @@ def tile_dcn_b_kernel(
                 normalise(nc, work, small, z, cols[:, row_gain + m : row_gain + m + 1], eps, h)
 
         for c, window in enumerate(all_windows[: D // P]):
-            term = work.tile([P, N], F32, name="term", tag="addend", bufs=3)
+            term = work.tile([P, N], F32, name="term")
             for half in HALVES:
                 nc.vector.tensor_mul(term[:, half], x0[c][:, half], s_ps[:, half])
             nc.vector.tensor_scalar_add(term[:], term[:], BC)
@@ -171,14 +170,8 @@ def tile_dcn_b_kernel(
             nc.sync.dma_start(out[c * P : (c + 1) * P, :], window[:])
 
         for m, window in enumerate(all_windows[D // P :]):
-            gain = cols[:, ROW_GAIN3 + m : ROW_GAIN3 + m + 1]
             z = linear(nc, psum, w3_sb, h2, m)
-            scaled = work.tile([P, N], F32, name="scaled", tag="addend", bufs=3)
-            if m == 0:
-                mean_var, scale = vector_moments(nc, small, z, gain, eps)
-                for half in HALVES:
-                    nc.vector.tensor_scalar(scaled[:, half], z[:, half], mean_var[:, 0:1], scale[:], SUBTRACT, MULT)
-            else:
-                normalise(nc, work, small, z, gain, eps, scaled)
+            scaled = work.tile([P, N], F32, name="scaled")
+            normalise(nc, work, small, z, cols[:, ROW_GAIN3 + m : ROW_GAIN3 + m + 1], eps, scaled)
             nc.vector.tensor_tensor(window[:].indirect(offsets[:]), scaled[:], shift_wide[m][:], ADD)
             nc.sync.dma_start(out[D + m * P : D + (m + 1) * P, :], window[:])

@@ -22,15 +22,19 @@ ROW_GAIN0, ROW_GAIN1, ROW_GAIN2, ROW_GAIN3, ROW_SHIFT3, ROW_WC = 0, 6, 14, 18, 2
 
 HALVES = (slice(0, BANK), slice(BANK, N))
 
+FIRST_BLOCKS = 2
+
+
+def accumulate(nc, z, weights_k, act, m, start, stop):
+    for half in HALVES:
+        nc.tensor.matmul(z[:, half], weights_k[:, m * P : (m + 1) * P], act[:, half], start=start, stop=stop)
+
 
 def linear(nc, psum, weights, acts, m):
     z = psum.tile([P, N], F32, name="z")
     last = len(acts) - 1
     for k, act in enumerate(acts):
-        for half in HALVES:
-            nc.tensor.matmul(
-                z[:, half], weights[k][:, m * P : (m + 1) * P], act[:, half], start=(k == 0), stop=(k == last)
-            )
+        accumulate(nc, z, weights[k], act, m, k == 0, k == last)
     return z
 
 
@@ -69,6 +73,7 @@ def tile_dcn_b_kernel(
     with (
         tc.tile_pool(name="held", bufs=1) as held,
         tc.tile_pool(name="acts", bufs=D // P) as acts,
+        tc.tile_pool(name="acts_wide", bufs=H1 // P) as acts_wide,
         tc.tile_pool(name="windows", bufs=C // P) as windows,
         tc.tile_pool(name="work", bufs=2) as work,
         tc.tile_pool(name="small", bufs=6) as small,
@@ -103,9 +108,10 @@ def tile_dcn_b_kernel(
         w1_all = held.tile([P, D // P, H1], BF16, name="w1_all")
         w2_all = held.tile([P, H1 // P, H2], BF16, name="w2_all")
         w3_all = held.tile([P, H2 // P, H3], BF16, name="w3_all")
-        nc.sync.dma_start(w1_all[:, :, : H1 // 2], w1.rearrange("(k p) h -> p k h", p=P)[:, :, : H1 // 2])
+        w1_blocks = w1.rearrange("(k p) h -> p k h", p=P)
+        nc.sync.dma_start(w1_all[:, :, : FIRST_BLOCKS * P], w1_blocks[:, :, : FIRST_BLOCKS * P])
         later_weights = (
-            (w1_all[:, :, H1 // 2 :], w1.rearrange("(k p) h -> p k h", p=P)[:, :, H1 // 2 :]),
+            (w1_all[:, :, FIRST_BLOCKS * P :], w1_blocks[:, :, FIRST_BLOCKS * P :]),
             (w2_all[:], w2.rearrange("(k p) h -> p k h", p=P)),
             (w3_all[:], w3.rearrange("(k p) h -> p k h", p=P)),
         )
@@ -143,7 +149,7 @@ def tile_dcn_b_kernel(
             nc.vector.tensor_scalar(bias[:], mean_var[:, 0:1], scale[:], -1.0, MULT, MULT)
             nc.scalar.activation(h0[k][:], x0[k][:], IDENTITY, scale=scale[:], bias=bias[:])
 
-            x0_bf = work.tile([P, N], BF16, name="x0_bf")
+            x0_bf = acts_wide.tile([P, N], BF16, name="x0_bf", tag="x0_bf_then_h1")
             nc.gpsimd.tensor_copy(x0_bf[:], x0[k][:])
             for half in HALVES:
                 nc.tensor.matmul(
@@ -154,12 +160,14 @@ def tile_dcn_b_kernel(
         for m, tile in enumerate(shift_wide):
             nc.gpsimd.tensor_copy(tile[:], cols[:, ROW_SHIFT3 + m : ROW_SHIFT3 + m + 1].to_broadcast([P, N]))
 
-        h1 = [held.tile([P, N], BF16, name=f"h1_{m}") for m in range(H1 // P)]
+        h1 = [acts_wide.tile([P, N], BF16, name=f"h1_{m}", tag="x0_bf_then_h1") for m in range(H1 // P)]
         h2 = [acts.tile([P, N], BF16, name=f"h2_{m}", tag="h0_then_h2") for m in range(H2 // P)]
-        for weights, inputs, outputs, row_gain in ((w1_sb, h0, h1, ROW_GAIN1), (w2_sb, h1, h2, ROW_GAIN2)):
-            for m, h in enumerate(outputs):
-                z = linear(nc, psum, weights, inputs, m)
-                normalise(nc, work, small, z, cols[:, row_gain + m : row_gain + m + 1], eps, h)
+        for m, h in enumerate(h1):
+            z = linear(nc, psum, w1_sb, h0, m)
+            normalise(nc, work, small, z, cols[:, ROW_GAIN1 + m : ROW_GAIN1 + m + 1], eps, h)
+        for m, h in enumerate(h2):
+            z = linear(nc, psum, w2_sb, h1, m)
+            normalise(nc, work, small, z, cols[:, ROW_GAIN2 + m : ROW_GAIN2 + m + 1], eps, h)
 
         for c, window in enumerate(all_windows[: D // P]):
             term = work.tile([P, N], F32, name="term")

@@ -18,16 +18,15 @@ BC = 0.25
 
 FLOPS = 2 * N * (D + D * H1 + H1 * H2 + H2 * H3)
 
-ROW_GAIN0, ROW_GAIN1, ROW_GAIN2, ROW_GAIN3, ROW_SHIFT3, ROW_WC = 0, 6, 14, 18, 20, 32
+ROW_GAIN0, ROW_WC = 0, 32
 
 HALVES = (slice(0, BANK), slice(BANK, N))
 
-FIRST_BLOCKS = 2
-
 
 def accumulate(nc, z, weights_k, act, m, start, stop):
+    blocks = weights_k.shape[1] // P
     for half in HALVES:
-        nc.tensor.matmul(z[:, half], weights_k[:, m * P : (m + 1) * P], act[:, half], start=start, stop=stop)
+        nc.tensor.matmul(z[:, half], weights_k[:, m::blocks], act[:, half], start=start, stop=stop)
 
 
 def linear(nc, psum, weights, acts, m):
@@ -89,15 +88,7 @@ def tile_dcn_b_kernel(
 
         staged = held.tile([P, P], F32, name="staged")
         nc.vector.memset(staged[:], 0.0)
-        for row, vector in (
-            (ROW_GAIN0, gain0),
-            (ROW_GAIN1, gain1),
-            (ROW_GAIN2, gain2),
-            (ROW_GAIN3, gain3),
-            (ROW_SHIFT3, shift3),
-        ):
-            as_rows = vector.rearrange("(r p) o -> r (p o)", p=P)
-            nc.sync.dma_start(staged[row : row + as_rows.shape[0], :], as_rows)
+        nc.sync.dma_start(staged[ROW_GAIN0 : ROW_GAIN0 + D // P, :], gain0.rearrange("(r p) o -> r (p o)", p=P))
         wc_rows = held.tile([P, P], BF16, name="wc_rows")
         nc.sync.dma_start(wc_rows[ROW_WC : ROW_WC + D // P, :], wc.rearrange("(r p) o -> r (p o)", p=P))
         nc.vector.tensor_copy(staged[ROW_WC : ROW_WC + D // P, :], wc_rows[ROW_WC : ROW_WC + D // P, :])
@@ -106,19 +97,30 @@ def tile_dcn_b_kernel(
             nc.sync.dma_start(x0[k][:], x0_rows[k])
 
         w1_all = held.tile([P, D // P, H1], BF16, name="w1_all")
+        nc.sync.dma_start(w1_all[:], w1.rearrange("(k p) h -> p k h", p=P))
+
+        gain_cols = []
+        for name, vector, rows in (("gain1", gain1, H1), ("gain2", gain2, H2), ("gain3", gain3, H3), ("shift3", shift3, H3)):
+            cols_of_vector = held.tile([P, rows // P], F32, name=f"{name}_cols")
+            nc.sync.dma_start(cols_of_vector[:], vector.rearrange("(p m) o -> p (m o)", p=P))
+            gain_cols.append(cols_of_vector)
+        gain1_cols, gain2_cols, gain3_cols, shift3_cols = gain_cols
+
         w2_all = held.tile([P, H1 // P, H2], BF16, name="w2_all")
         w3_all = held.tile([P, H2 // P, H3], BF16, name="w3_all")
-        w1_blocks = w1.rearrange("(k p) h -> p k h", p=P)
-        nc.sync.dma_start(w1_all[:, :, : FIRST_BLOCKS * P], w1_blocks[:, :, : FIRST_BLOCKS * P])
         later_weights = (
-            (w1_all[:, :, FIRST_BLOCKS * P :], w1_blocks[:, :, FIRST_BLOCKS * P :]),
-            (w2_all[:], w2.rearrange("(k p) h -> p k h", p=P)),
-            (w3_all[:], w3.rearrange("(k p) h -> p k h", p=P)),
+            (w2_all[:], w2.rearrange("(p k) h -> p k h", p=P)),
+            (w3_all[:], w3.rearrange("(p k) h -> p k h", p=P)),
         )
+        base_blocks = [base[c * P : (c + 1) * P, :] for c in range(D // P)]
+        out_blocks = [out[c * P : (c + 1) * P, :] for c in range(D // P)]
+        for m in range(H3 // P):
+            base_blocks.append(base[D:C, :].rearrange("(p m) s -> m p s", p=P)[m])
+            out_blocks.append(out[D:C, :].rearrange("(p m) s -> m p s", p=P)[m])
         all_windows = []
-        for c in range(C // P):
+        for c, rows_of_base in enumerate(base_blocks):
             window = windows.tile([P, S], F32, name="window")
-            nc.sync.dma_start(window[:], base[c * P : (c + 1) * P, :])
+            nc.sync.dma_start(window[:], rows_of_base)
             all_windows.append(window)
             if c < len(later_weights):
                 nc.sync.dma_start(later_weights[c][0], later_weights[c][1])
@@ -158,16 +160,16 @@ def tile_dcn_b_kernel(
 
         shift_wide = [held.tile([P, N], F32, name=f"shift_wide_{m}") for m in range(H3 // P)]
         for m, tile in enumerate(shift_wide):
-            nc.gpsimd.tensor_copy(tile[:], cols[:, ROW_SHIFT3 + m : ROW_SHIFT3 + m + 1].to_broadcast([P, N]))
+            nc.gpsimd.tensor_copy(tile[:], shift3_cols[:, m : m + 1].to_broadcast([P, N]))
 
         h1 = [acts_wide.tile([P, N], BF16, name=f"h1_{m}", tag="x0_bf_then_h1") for m in range(H1 // P)]
         h2 = [acts.tile([P, N], BF16, name=f"h2_{m}", tag="h0_then_h2") for m in range(H2 // P)]
         for m, h in enumerate(h1):
             z = linear(nc, psum, w1_sb, h0, m)
-            normalise(nc, work, small, z, cols[:, ROW_GAIN1 + m : ROW_GAIN1 + m + 1], eps, h)
+            normalise(nc, work, small, z, gain1_cols[:, m : m + 1], eps, h)
         for m, h in enumerate(h2):
             z = linear(nc, psum, w2_sb, h1, m)
-            normalise(nc, work, small, z, cols[:, ROW_GAIN2 + m : ROW_GAIN2 + m + 1], eps, h)
+            normalise(nc, work, small, z, gain2_cols[:, m : m + 1], eps, h)
 
         for c, window in enumerate(all_windows[: D // P]):
             term = work.tile([P, N], F32, name="term")
@@ -175,11 +177,11 @@ def tile_dcn_b_kernel(
                 nc.vector.tensor_mul(term[:, half], x0[c][:, half], s_ps[:, half])
             nc.vector.tensor_scalar_add(term[:], term[:], BC)
             nc.vector.tensor_tensor(window[:].indirect(offsets[:]), term[:], x0[c][:], ADD)
-            nc.sync.dma_start(out[c * P : (c + 1) * P, :], window[:])
+            nc.sync.dma_start(out_blocks[c], window[:])
 
         for m, window in enumerate(all_windows[D // P :]):
             z = linear(nc, psum, w3_sb, h2, m)
             scaled = work.tile([P, N], F32, name="scaled")
-            normalise(nc, work, small, z, cols[:, ROW_GAIN3 + m : ROW_GAIN3 + m + 1], eps, scaled)
+            normalise(nc, work, small, z, gain3_cols[:, m : m + 1], eps, scaled)
             nc.vector.tensor_tensor(window[:].indirect(offsets[:]), scaled[:], shift_wide[m][:], ADD)
-            nc.sync.dma_start(out[D + m * P : D + (m + 1) * P, :], window[:])
+            nc.sync.dma_start(out_blocks[D // P + m], window[:])

@@ -102,7 +102,7 @@ def tile_dcn_b_kernel(
         gain_cols = []
         for name, vector, rows in (("gain1", gain1, H1), ("gain2", gain2, H2), ("gain3", gain3, H3), ("shift3", shift3, H3)):
             cols_of_vector = held.tile([P, rows // P], F32, name=f"{name}_cols")
-            nc.sync.dma_start(cols_of_vector[:], vector.rearrange("(p m) o -> p (m o)", p=P))
+            nc.scalar.dma_start(cols_of_vector[:], vector.rearrange("(p m) o -> p (m o)", p=P))
             gain_cols.append(cols_of_vector)
         gain1_cols, gain2_cols, gain3_cols, shift3_cols = gain_cols
 

@@ -51,7 +51,7 @@ def vector_moments(nc, small, v, gain, eps):
 
 
 def normalise(nc, work, small, z, gain, eps, h):
-    squares = work.tile([P, N], BF16, name="squares", bufs=1)
+    squares = work.tile([P, N], BF16, name="squares")
     sums = small.tile([P, 2], F32, name="sums")
     for i, half in enumerate(HALVES):
         nc.scalar.activation(squares[:, half], z[:, half], SQUARE, accum_out=sums[:, i : i + 1])
@@ -71,10 +71,11 @@ def tile_dcn_b_kernel(
     nc = tc.nc
     with (
         tc.tile_pool(name="held", bufs=1) as held,
+        tc.tile_pool(name="rows32", bufs=2 * (D // P)) as rows32,
         tc.tile_pool(name="acts", bufs=D // P) as acts,
         tc.tile_pool(name="acts_wide", bufs=H1 // P) as acts_wide,
         tc.tile_pool(name="windows", bufs=C // P) as windows,
-        tc.tile_pool(name="work", bufs=2) as work,
+        tc.tile_pool(name="work", bufs=1) as work,
         tc.tile_pool(name="small", bufs=6) as small,
         tc.psum_pool(name="psum", bufs=3) as psum,
         tc.psum_pool(name="psum_s", bufs=1) as psum_s,
@@ -82,7 +83,10 @@ def tile_dcn_b_kernel(
         offsets = held.tile([P, N // 16], U16, name="offsets")
         nc.sync.dma_start(offsets[:], offs)
 
-        x0 = [held.tile([P, N], F32, name=f"x0_{k}") for k in range(D // P)]
+        x0, x0_plus = [], []
+        for k in range(D // P):
+            x0.append(rows32.tile([P, N], F32, name=f"x0_{k}", tag="rows32"))
+            x0_plus.append(rows32.tile([P, N], F32, name=f"x0_plus_{k}", tag="rows32"))
         x0_rows = [emb[k * P : (k + 1) * P, :] for k in range(CE // P)] + [dense]
         nc.sync.dma_start(x0[0][:], x0_rows[0])
 
@@ -158,9 +162,8 @@ def tile_dcn_b_kernel(
                     s_ps[:, half], wc_wide[:, k, :], x0_bf[:, half], start=(k == 0), stop=(k == D // P - 1)
                 )
 
-        shift_wide = [held.tile([P, N], F32, name=f"shift_wide_{m}") for m in range(H3 // P)]
-        for m, tile in enumerate(shift_wide):
-            nc.gpsimd.tensor_copy(tile[:], shift3_cols[:, m : m + 1].to_broadcast([P, N]))
+        for k in range(D // P):
+            nc.vector.tensor_scalar_add(x0_plus[k][:], x0[k][:], BC)
 
         h1 = [acts_wide.tile([P, N], BF16, name=f"h1_{m}", tag="x0_bf_then_h1") for m in range(H1 // P)]
         h2 = [acts.tile([P, N], BF16, name=f"h2_{m}", tag="h0_then_h2") for m in range(H2 // P)]
@@ -172,16 +175,21 @@ def tile_dcn_b_kernel(
             normalise(nc, work, small, z, gain2_cols[:, m : m + 1], eps, h)
 
         for c, window in enumerate(all_windows[: D // P]):
-            term = work.tile([P, N], F32, name="term")
+            product = work.tile([P, N], F32, name="product")
             for half in HALVES:
-                nc.vector.tensor_mul(term[:, half], x0[c][:, half], s_ps[:, half])
-            nc.vector.tensor_scalar_add(term[:], term[:], BC)
-            nc.vector.tensor_tensor(window[:].indirect(offsets[:]), term[:], x0[c][:], ADD)
+                nc.vector.tensor_mul(product[:, half], x0[c][:, half], s_ps[:, half])
+            nc.vector.tensor_tensor(window[:].indirect(offsets[:]), product[:], x0_plus[c][:], ADD)
             nc.sync.dma_start(out_blocks[c], window[:])
+
+        shift_wide = []
+        for m in range(H3 // P):
+            spread = rows32.tile([P, N], F32, name=f"shift_wide_{m}", tag="rows32")
+            nc.vector.tensor_copy(spread[:], shift3_cols[:, m : m + 1].to_broadcast([P, N]))
+            shift_wide.append(spread)
 
         for m, window in enumerate(all_windows[D // P :]):
             z = linear(nc, psum, w3_sb, h2, m)
-            scaled = work.tile([P, N], F32, name="scaled")
+            scaled = rows32.tile([P, N], F32, name="scaled", tag="rows32")
             normalise(nc, work, small, z, gain3_cols[:, m : m + 1], eps, scaled)
             nc.vector.tensor_tensor(window[:].indirect(offsets[:]), scaled[:], shift_wide[m][:], ADD)
             nc.sync.dma_start(out_blocks[D // P + m], window[:])

@@ -22,6 +22,8 @@ ROW_GAIN0, ROW_WC = 0, 32
 
 HALVES = (slice(0, BANK), slice(BANK, N))
 
+W1_BLOCKS_A_LOAD = 3
+
 
 def accumulate(nc, z, weights_k, act, m, start, stop):
     blocks = weights_k.shape[1] // P
@@ -100,8 +102,12 @@ def tile_dcn_b_kernel(
         for k in range(1, D // P):
             nc.sync.dma_start(x0[k][:], x0_rows[k])
 
-        w1_all = held.tile([P, D // P, H1], BF16, name="w1_all")
-        nc.sync.dma_start(w1_all[:], w1.rearrange("(k p) h -> p k h", p=P))
+        w1_blocks = w1.rearrange("(k p) h -> p k h", p=P)
+        w1_sb = []
+        for first in range(0, D // P, W1_BLOCKS_A_LOAD):
+            w1_part = held.tile([P, W1_BLOCKS_A_LOAD, H1], BF16, name=f"w1_part_{first}")
+            nc.sync.dma_start(w1_part[:], w1_blocks[:, first : first + W1_BLOCKS_A_LOAD, :])
+            w1_sb.extend(w1_part[:, k, :] for k in range(W1_BLOCKS_A_LOAD))
 
         gain_cols = []
         for name, vector, rows in (("gain1", gain1, H1), ("gain2", gain2, H2), ("gain3", gain3, H3), ("shift3", shift3, H3)):
@@ -128,7 +134,6 @@ def tile_dcn_b_kernel(
             all_windows.append(window)
             if c < len(later_weights):
                 nc.sync.dma_start(later_weights[c][0], later_weights[c][1])
-        w1_sb = [w1_all[:, k, :] for k in range(D // P)]
         w2_sb = [w2_all[:, k, :] for k in range(H1 // P)]
         w3_sb = [w3_all[:, k, :] for k in range(H2 // P)]
 
@@ -142,10 +147,8 @@ def tile_dcn_b_kernel(
         eps = held.tile([P, 1], F32, name="eps")
         nc.vector.memset(eps[:], EPS)
 
-        wc_wide = held.tile([P, D // P, P], BF16, name="wc_wide")
-        nc.vector.tensor_copy(
-            wc_wide[:], cols[:, ROW_WC : ROW_WC + D // P].unsqueeze(2).to_broadcast([P, D // P, P])
-        )
+        wc_cols = held.tile([P, D // P], BF16, name="wc_cols")
+        nc.vector.tensor_copy(wc_cols[:], cols[:, ROW_WC : ROW_WC + D // P])
 
         h0 = [acts.tile([P, N], BF16, name=f"h0_{k}", tag="h0_then_h2") for k in range(D // P)]
         s_ps = psum_s.tile([P, N], F32, name="s_ps")
@@ -159,7 +162,11 @@ def tile_dcn_b_kernel(
             nc.gpsimd.tensor_copy(x0_bf[:], x0[k][:])
             for half in HALVES:
                 nc.tensor.matmul(
-                    s_ps[:, half], wc_wide[:, k, :], x0_bf[:, half], start=(k == 0), stop=(k == D // P - 1)
+                    s_ps[:, half],
+                    wc_cols[:, k : k + 1].to_broadcast([P, P]),
+                    x0_bf[:, half],
+                    start=(k == 0),
+                    stop=(k == D // P - 1),
                 )
 
         for k in range(D // P):

@@ -73,7 +73,7 @@ def tile_dcn_b_kernel(
     nc = tc.nc
     with (
         tc.tile_pool(name="held", bufs=1) as held,
-        tc.tile_pool(name="rows32", bufs=2 * (D // P)) as rows32,
+        tc.tile_pool(name="rows32", bufs=D // P + 2) as rows32,
         tc.tile_pool(name="acts", bufs=D // P) as acts,
         tc.tile_pool(name="acts_wide", bufs=H1 // P) as acts_wide,
         tc.tile_pool(name="windows", bufs=C // P) as windows,
@@ -85,12 +85,12 @@ def tile_dcn_b_kernel(
         offsets = held.tile([P, N // 16], U16, name="offsets")
         nc.sync.dma_start(offsets[:], offs)
 
-        x0, x0_plus = [], []
-        for k in range(D // P):
-            x0.append(rows32.tile([P, N], F32, name=f"x0_{k}", tag="rows32"))
-            x0_plus.append(rows32.tile([P, N], F32, name=f"x0_plus_{k}", tag="rows32"))
-        x0_rows = [emb[k * P : (k + 1) * P, :] for k in range(CE // P)] + [dense]
-        nc.sync.dma_start(x0[0][:], x0_rows[0])
+        x0_first = rows32.tile([P, N], F32, name="x0_first", tag="rows32")
+        x0_pairs = [held.tile([P, 2, N], F32, name=f"x0_pair_{i}") for i in range(2)]
+        x0_last = rows32.tile([P, N], F32, name="x0_last", tag="rows32")
+        x0 = [x0_first[:]] + [pair[:, i, :] for pair in x0_pairs for i in range(2)] + [x0_last[:]]
+        x0_plus = [rows32.tile([P, N], F32, name=f"x0_plus_{k}", tag="rows32") for k in range(D // P)]
+        nc.sync.dma_start(x0_first[:], emb[0:P, :])
 
         staged = held.tile([P, P], F32, name="staged")
         nc.vector.memset(staged[:], 0.0)
@@ -99,8 +99,10 @@ def tile_dcn_b_kernel(
         nc.sync.dma_start(wc_rows[ROW_WC : ROW_WC + D // P, :], wc.rearrange("(r p) o -> r (p o)", p=P))
         nc.vector.tensor_copy(staged[ROW_WC : ROW_WC + D // P, :], wc_rows[ROW_WC : ROW_WC + D // P, :])
 
-        for k in range(1, D // P):
-            nc.sync.dma_start(x0[k][:], x0_rows[k])
+        for i, pair in enumerate(x0_pairs):
+            first_row = (1 + 2 * i) * P
+            nc.sync.dma_start(pair[:], emb[first_row : first_row + 2 * P, :].rearrange("(k p) n -> p k n", p=P))
+        nc.sync.dma_start(x0_last[:], dense)
 
         w1_blocks = w1.rearrange("(k p) h -> p k h", p=P)
         w1_sb = []
@@ -156,10 +158,10 @@ def tile_dcn_b_kernel(
             mean_var, scale = vector_moments(nc, small, x0[k], cols[:, ROW_GAIN0 + k : ROW_GAIN0 + k + 1], eps)
             bias = small.tile([P, 1], F32, name="bias0")
             nc.vector.tensor_scalar(bias[:], mean_var[:, 0:1], scale[:], -1.0, MULT, MULT)
-            nc.scalar.activation(h0[k][:], x0[k][:], IDENTITY, scale=scale[:], bias=bias[:])
+            nc.scalar.activation(h0[k][:], x0[k], IDENTITY, scale=scale[:], bias=bias[:])
 
             x0_bf = acts_wide.tile([P, N], BF16, name="x0_bf", tag="x0_bf_then_h1")
-            nc.gpsimd.tensor_copy(x0_bf[:], x0[k][:])
+            nc.gpsimd.tensor_copy(x0_bf[:], x0[k])
             for half in HALVES:
                 nc.tensor.matmul(
                     s_ps[:, half],
@@ -170,7 +172,7 @@ def tile_dcn_b_kernel(
                 )
 
         for k in range(D // P):
-            nc.vector.tensor_scalar_add(x0_plus[k][:], x0[k][:], BC)
+            nc.vector.tensor_scalar_add(x0_plus[k][:], x0[k], BC)
 
         h1 = [acts_wide.tile([P, N], BF16, name=f"h1_{m}", tag="x0_bf_then_h1") for m in range(H1 // P)]
         h2 = [acts.tile([P, N], BF16, name=f"h2_{m}", tag="h0_then_h2") for m in range(H2 // P)]

import concourse.mybir as mybir
from concourse.masks import make_identity

F32, BF16, U16 = mybir.dt.float32, mybir.dt.bfloat16, mybir.dt.uint16
ADD, MULT = mybir.AluOpType.add, mybir.AluOpType.mult
IDENTITY = mybir.ActivationFunctionType.Identity
SQUARE = mybir.ActivationFunctionType.Square
ABS_RSQRT = mybir.ActivationFunctionType.Abs_reciprocal_sqrt

P = 128
N = 1024
S = 4096
BANK = 512
CE, D, H1, H2, H3 = 640, 768, 1024, 512, 256
C = D + H3
EPS = 1e-5
BC = 0.25

FLOPS = 2 * N * (D + D * H1 + H1 * H2 + H2 * H3)

ROW_GAIN0, ROW_WC = 0, 32

HALVES = (slice(0, BANK), slice(BANK, N))

W1_BLOCKS_A_LOAD = 3


def accumulate(nc, z, weights_k, act, m, start, stop):
    blocks = weights_k.shape[1] // P
    for half in HALVES:
        nc.tensor.matmul(z[:, half], weights_k[:, m::blocks], act[:, half], start=start, stop=stop)


def linear(nc, psum, weights, acts, m):
    z = psum.tile([P, N], F32, name="z")
    last = len(acts) - 1
    for k, act in enumerate(acts):
        accumulate(nc, z, weights[k], act, m, k == 0, k == last)
    return z


def vector_moments(nc, small, v, gain, eps):
    stats = small.tile([P, 2, 6], F32, name="stats")
    for i, half in enumerate(HALVES):
        nc.vector.bn_stats(stats[:, i, :], v[:, half])
    mean_var = small.tile([P, 2], F32, name="mean_var")
    nc.vector.bn_aggr(mean_var[:], stats[:].rearrange("p a b -> p (a b)"))
    rstd = small.tile([P, 1], F32, name="rstd_v")
    nc.scalar.activation(rstd[:], mean_var[:, 1:2], ABS_RSQRT, bias=eps[:])
    scale = small.tile([P, 1], F32, name="scale_v")
    nc.vector.tensor_scalar_mul(scale[:], rstd[:], gain)
    return mean_var, scale


def normalise(nc, work, small, z, gain, eps, h):
    squares = work.tile([P, N], BF16, name="squares")
    sums = small.tile([P, 2], F32, name="sums")
    for i, half in enumerate(HALVES):
        nc.scalar.activation(squares[:, half], z[:, half], SQUARE, accum_out=sums[:, i : i + 1])
    second = small.tile([P, 1], F32, name="second")
    nc.scalar.activation(second[:], sums[:, 1:2], IDENTITY, scale=1.0 / N, bias=eps[:])
    rstd = small.tile([P, 1], F32, name="rstd")
    nc.scalar.activation(rstd[:], sums[:, 0:1], ABS_RSQRT, scale=1.0 / N, bias=second[:])
    scale = small.tile([P, 1], F32, name="scale")
    nc.scalar.activation(scale[:], rstd[:], IDENTITY, scale=gain)
    for half in HALVES:
        nc.scalar.activation(h[:, half], z[:, half], IDENTITY, scale=scale[:])


def tile_dcn_b_kernel(
    tc, base, emb, dense, wc, gain0, w1, gain1, w2, gain2, w3, gain3, shift3, offs, out
):
    nc = tc.nc
    with (
        tc.tile_pool(name="held", bufs=1) as held,
        tc.tile_pool(name="rows32", bufs=D // P + 2) as rows32,
        tc.tile_pool(name="acts", bufs=D // P) as acts,
        tc.tile_pool(name="acts_wide", bufs=H1 // P) as acts_wide,
        tc.tile_pool(name="windows", bufs=C // P) as windows,
        tc.tile_pool(name="work", bufs=1) as work,
        tc.tile_pool(name="small", bufs=6) as small,
        tc.psum_pool(name="psum", bufs=3) as psum,
        tc.psum_pool(name="psum_s", bufs=1) as psum_s,
    ):
        offsets = held.tile([P, N // 16], U16, name="offsets")
        nc.sync.dma_start(offsets[:], offs)

        x0_first = rows32.tile([P, N], F32, name="x0_first", tag="rows32")
        x0_pairs = [held.tile([P, 2, N], F32, name=f"x0_pair_{i}") for i in range(2)]
        x0_last = rows32.tile([P, N], F32, name="x0_last", tag="rows32")
        x0 = [x0_first[:]] + [pair[:, i, :] for pair in x0_pairs for i in range(2)] + [x0_last[:]]
        x0_plus = [rows32.tile([P, N], F32, name=f"x0_plus_{k}", tag="rows32") for k in range(D // P)]
        nc.sync.dma_start(x0_first[:], emb[0:P, :])

        staged = held.tile([P, P], F32, name="staged")
        nc.vector.memset(staged[:], 0.0)
        nc.sync.dma_start(staged[ROW_GAIN0 : ROW_GAIN0 + D // P, :], gain0.rearrange("(r p) o -> r (p o)", p=P))
        wc_rows = held.tile([P, P], BF16, name="wc_rows")
        nc.sync.dma_start(wc_rows[ROW_WC : ROW_WC + D // P, :], wc.rearrange("(r p) o -> r (p o)", p=P))
        nc.vector.tensor_copy(staged[ROW_WC : ROW_WC + D // P, :], wc_rows[ROW_WC : ROW_WC + D // P, :])

        for i, pair in enumerate(x0_pairs):
            first_row = (1 + 2 * i) * P
            nc.sync.dma_start(pair[:], emb[first_row : first_row + 2 * P, :].rearrange("(k p) n -> p k n", p=P))
        nc.sync.dma_start(x0_last[:], dense)

        w1_blocks = w1.rearrange("(k p) h -> p k h", p=P)
        w1_sb = []
        for first in range(0, D // P, W1_BLOCKS_A_LOAD):
            w1_part = held.tile([P, W1_BLOCKS_A_LOAD, H1], BF16, name=f"w1_part_{first}")
            nc.sync.dma_start(w1_part[:], w1_blocks[:, first : first + W1_BLOCKS_A_LOAD, :])
            w1_sb.extend(w1_part[:, k, :] for k in range(W1_BLOCKS_A_LOAD))

        gain_cols = []
        for name, vector, rows in (("gain1", gain1, H1), ("gain2", gain2, H2), ("gain3", gain3, H3), ("shift3", shift3, H3)):
            cols_of_vector = held.tile([P, rows // P], F32, name=f"{name}_cols")
            nc.scalar.dma_start(cols_of_vector[:], vector.rearrange("(p m) o -> p (m o)", p=P))
            gain_cols.append(cols_of_vector)
        gain1_cols, gain2_cols, gain3_cols, shift3_cols = gain_cols

        w2_all = held.tile([P, H1 // P, H2], BF16, name="w2_all")
        w3_all = held.tile([P, H2 // P, H3], BF16, name="w3_all")
        later_weights = (
            (w2_all[:], w2.rearrange("(p k) h -> p k h", p=P)),
            (w3_all[:], w3.rearrange("(p k) h -> p k h", p=P)),
        )
        base_blocks = [base[c * P : (c + 1) * P, :] for c in range(D // P)]
        out_blocks = [out[c * P : (c + 1) * P, :] for c in range(D // P)]
        for m in range(H3 // P):
            base_blocks.append(base[D:C, :].rearrange("(p m) s -> m p s", p=P)[m])
            out_blocks.append(out[D:C, :].rearrange("(p m) s -> m p s", p=P)[m])
        all_windows = []
        for c, rows_of_base in enumerate(base_blocks):
            window = windows.tile([P, S], F32, name="window")
            nc.sync.dma_start(window[:], rows_of_base)
            all_windows.append(window)
            if c < len(later_weights):
                nc.sync.dma_start(later_weights[c][0], later_weights[c][1])
        w2_sb = [w2_all[:, k, :] for k in range(H1 // P)]
        w3_sb = [w3_all[:, k, :] for k in range(H2 // P)]

        identity = held.tile([P, P], F32, name="identity")
        make_identity(nc, identity[:])
        cols_ps = psum.tile([P, P], F32, name="cols_ps", tag="z")
        nc.tensor.transpose(cols_ps[:], staged[:], identity[:])
        cols = held.tile([P, P], F32, name="cols")
        nc.vector.tensor_copy(cols[:], cols_ps[:])

        eps = held.tile([P, 1], F32, name="eps")
        nc.vector.memset(eps[:], EPS)

        wc_cols = held.tile([P, D // P], BF16, name="wc_cols")
        nc.vector.tensor_copy(wc_cols[:], cols[:, ROW_WC : ROW_WC + D // P])

        h0 = [acts.tile([P, N], BF16, name=f"h0_{k}", tag="h0_then_h2") for k in range(D // P)]
        s_ps = psum_s.tile([P, N], F32, name="s_ps")
        for k in range(D // P):
            mean_var, scale = vector_moments(nc, small, x0[k], cols[:, ROW_GAIN0 + k : ROW_GAIN0 + k + 1], eps)
            bias = small.tile([P, 1], F32, name="bias0")
            nc.vector.tensor_scalar(bias[:], mean_var[:, 0:1], scale[:], -1.0, MULT, MULT)
            nc.scalar.activation(h0[k][:], x0[k], IDENTITY, scale=scale[:], bias=bias[:])

            x0_bf = acts_wide.tile([P, N], BF16, name="x0_bf", tag="x0_bf_then_h1")
            nc.gpsimd.tensor_copy(x0_bf[:], x0[k])
            for half in HALVES:
                nc.tensor.matmul(
                    s_ps[:, half],
                    wc_cols[:, k : k + 1].to_broadcast([P, P]),
                    x0_bf[:, half],
                    start=(k == 0),
                    stop=(k == D // P - 1),
                )

        for k in range(D // P):
            nc.vector.tensor_scalar_add(x0_plus[k][:], x0[k], BC)

        h1 = [acts_wide.tile([P, N], BF16, name=f"h1_{m}", tag="x0_bf_then_h1") for m in range(H1 // P)]
        h2 = [acts.tile([P, N], BF16, name=f"h2_{m}", tag="h0_then_h2") for m in range(H2 // P)]
        for m, h in enumerate(h1):
            z = linear(nc, psum, w1_sb, h0, m)
            normalise(nc, work, small, z, gain1_cols[:, m : m + 1], eps, h)
        for m, h in enumerate(h2):
            z = linear(nc, psum, w2_sb, h1, m)
            normalise(nc, work, small, z, gain2_cols[:, m : m + 1], eps, h)

        for c, window in enumerate(all_windows[: D // P]):
            product = work.tile([P, N], F32, name="product")
            for half in HALVES:
                nc.vector.tensor_mul(product[:, half], x0[c][:, half], s_ps[:, half])
            nc.vector.tensor_tensor(window[:].indirect(offsets[:]), product[:], x0_plus[c][:], ADD)
            nc.sync.dma_start(out_blocks[c], window[:])

        shift_wide = []
        for m in range(H3 // P):
            spread = rows32.tile([P, N], F32, name=f"shift_wide_{m}", tag="rows32")
            nc.vector.tensor_copy(spread[:], shift3_cols[:, m : m + 1].to_broadcast([P, N]))
            shift_wide.append(spread)

        for m, window in enumerate(all_windows[D // P :]):
            z = linear(nc, psum, w3_sb, h2, m)
            scaled = rows32.tile([P, N], F32, name="scaled", tag="rows32")
            normalise(nc, work, small, z, gain3_cols[:, m : m + 1], eps, scaled)
            nc.vector.tensor_tensor(window[:].indirect(offsets[:]), scaled[:], shift_wide[m][:], ADD)
            nc.sync.dma_start(out_blocks[D // P + m], window[:])
